import numpy as np
import ml_dtypes


def mxq(x, axis, fmt="e4m3"):
    dtype, down = {"e4m3": (ml_dtypes.float8_e4m3fn, 7), "e5m2": (ml_dtypes.float8_e5m2, 14)}[fmt]
    v = np.moveaxis(np.asarray(x, np.float32).astype(ml_dtypes.bfloat16).astype(np.float64), axis, -1)
    blocks = v.reshape(v.shape[:-1] + (-1, 32))
    amax = np.abs(blocks).max(-1, keepdims=True)
    byte = np.maximum(np.where(amax > 0, np.frexp(amax)[1] - 1 + 127, 0) - down, 1)
    scale = np.exp2(byte - 127.0)
    codes = (blocks / scale).astype(np.float32).astype(dtype).astype(np.float64)
    return np.moveaxis((codes * scale).reshape(v.shape), -1, axis)


WIDE = False


def mx_kscale(k):
    if not WIDE:
        return np.ones(k)
    levels = np.array([10, -10, 5, -5, 0])
    a = np.random.permutation(np.resize(levels, k // 512 * 4)).reshape(k // 512, 4)
    idx = np.arange(k)
    return np.exp2(a[idx // 512, idx % 128 // 32])


BF16 = ml_dtypes.bfloat16


def bf(x):
    return np.asarray(x, np.float32).astype(BF16)


def f64(x):
    return np.asarray(x).astype(np.float64)


E2M1 = np.array([0.0, 0.5, 1.0, 1.5, 2.0, 3.0, 4.0, 6.0, -0.0, -0.5, -1.0, -1.5, -2.0, -3.0, -4.0, -6.0])


def pack_weight(w, fmt):
    k, n = w.shape
    w = f64(bf(w)).reshape(k // 32, 32, n)
    amax = np.abs(w).max(1)
    if fmt == "e4m3":
        byte = np.frexp(amax)[1] - 1 + 127 - 7
    else:
        mant, ex = np.frexp(amax / 6.0)
        byte = np.where(mant > 0.5, ex, ex - 1) + 127
    byte = np.clip(np.where(amax > 0, byte, 1), 1, 254)
    scaled = (w * np.exp2(127.0 - byte)[:, None, :]).reshape(k, n).astype(np.float32)
    by_word = np.ascontiguousarray(scaled.reshape(k // 512, 128, 4, n).transpose(0, 1, 3, 2))
    if fmt == "e4m3":
        words = by_word.astype(ml_dtypes.float8_e4m3fn).view(np.uint8)
    else:
        c = by_word.astype(ml_dtypes.float4_e2m1fn).view(np.uint8) & 0xF
        words = c[..., 0::2] | (c[..., 1::2] << 4)
    return np.ascontiguousarray(words), np.ascontiguousarray(byte.astype(np.uint8).reshape(k // 512, 16, n))


def unpack_weight(words, scales, fmt):
    g, p, n, _ = words.shape
    if fmt == "e4m3":
        vals = np.ascontiguousarray(words).view(ml_dtypes.float8_e4m3fn).astype(np.float64)
    else:
        nib = np.empty((g, p, n, 4), np.uint8)
        nib[..., 0::2] = words & 0xF
        nib[..., 1::2] = words >> 4
        vals = E2M1[nib]
    vals = vals * np.repeat(np.exp2(scales.astype(np.float64) - 127.0), 8, axis=1)[..., None]
    return vals.transpose(0, 1, 3, 2).reshape(g * 512, n)

def pack4(w):
    words, scales = pack_weight(w, "e2m1")
    return words.reshape(words.shape[0], 128, -1), scales


def unpack4(words, scales):
    return unpack_weight(words.reshape(words.shape[0], 128, -1, 2), scales, "e2m1")


B, F_IN, H, D, N = 768, 768, 512, 512, 128
C = 3.0
SQRT_C = np.sqrt(C)
MIN_NORM = 1e-15
EPS = 1e-5
TEMP = 0.07


def artanh(v):
    return 0.5 * np.log((1.0 + v) / (1.0 - v))


def expmap0(u):
    un = np.maximum(np.sqrt((u * u).sum(-1, keepdims=True)), MIN_NORM)
    return np.tanh(SQRT_C * un) * u / (SQRT_C * un)


def profile():
    d = 1.0 / np.sqrt(1.0 + np.arange(D))
    return d / np.sqrt((d * d).sum())


def setup_inputs():
    s = mx_kscale(H)
    d = profile()
    g = np.random.standard_normal((N, D)) * d
    h_mlp = bf(np.random.standard_normal((B, H)) * 0.65 * s)
    W3_words, W3_scales = pack4(np.random.standard_normal((H, D)) * 0.8 / np.sqrt(H) * d / s[:, None])
    b3 = bf(np.random.standard_normal(D) * 0.2 * d)
    return {"h_mlp": h_mlp,
            "W3_words": W3_words,
            "W3_scales": W3_scales,
            "b3": b3,
            "prototypes": bf(g / np.sqrt((g * g).sum(1, keepdims=True)) * 0.95 / C)}


def reference(h_mlp, W3_words, W3_scales, b3, prototypes):
    p = f64(prototypes)
    u = (mxq(f64(h_mlp), 1, "e4m3") @ unpack4(W3_words, W3_scales)) + f64(b3)
    hyp = expmap0(u)
    A = (p * p).sum(-1)
    Bn = (hyp * hyp).sum(-1)
    P = mxq(hyp, 1, "e4m3") @ mxq(p, 1, "e4m3").T
    alpha = 1.0 - 2.0 * C * P + C * Bn[:, None]
    beta = 1.0 - C * A[None, :]
    denom = np.maximum(1.0 - 2.0 * C * P + (C * C) * A[None, :] * Bn[:, None], MIN_NORM)
    num_sq = alpha * alpha * A[None, :] + beta * beta * Bn[:, None] - 2.0 * alpha * beta * P
    mnorm = np.sqrt(np.maximum(num_sq, MIN_NORM)) / denom
    arg = np.minimum(SQRT_C * mnorm, 1.0 - EPS)
    dist = (2.0 / SQRT_C) * artanh(arg)
    return -dist / TEMP, hyp

@@ -1,0 +1,417 @@
+import math
+from contextlib import ExitStack
+
+import concourse.mybir as mybir
+from concourse.masks import make_identity
+
+F32 = mybir.dt.float32
+BF16 = mybir.dt.bfloat16
+I32 = mybir.dt.int32
+U32 = mybir.dt.uint32
+U8 = mybir.dt.uint8
+FP8X4 = mybir.dt.float8_e4m3fn_x4
+FP4X4 = mybir.dt.float4_e2m1fn_x4
+ALU = mybir.AluOpType
+ACT = mybir.ActivationFunctionType
+
+P = 128
+PACK = 4
+B, H, D, N = 768, 512, 512, 128
+TILES = B // P
+PAIR = 2
+PAIRS = TILES // PAIR
+BANKS = 8
+
+C = 3.0
+SQRT_C = math.sqrt(C)
+MIN_NORM = 1e-15
+EPS = 1e-5
+TEMP = 0.07
+BALL_EDGE = 1e-9
+LOGIT_SCALE = -2.0 / (SQRT_C * TEMP)
+ARTANH_MAX = 0.5 * math.log((2.0 - EPS) / EPS)
+
+FLOPS = 2 * B * H * D + 2 * B * D * N
+
+
+def tile_hyperbolicuniform_pa_s_kernel(
+    tc, h_mlp, W3_words, W3_scales, b3, prototypes, out_0, out_1
+):
+    nc = tc.nc
+    h_rows = h_mlp.rearrange("(p t) k -> p t k", t=TILES)
+    logit_rows = out_0.rearrange("(p t) n -> p t n", t=TILES)
+    hyp_rows = out_1.rearrange("(p t) d -> p t d", t=TILES)
+
+    def tiles_of(j):
+        return slice(PAIR * j, PAIR * (j + 1))
+
+    with ExitStack() as ctx:
+        keep = ctx.enter_context(tc.tile_pool(name="keep", bufs=1))
+        scratch = ctx.enter_context(tc.tile_pool(name="scratch", bufs=4))
+        psum = ctx.enter_context(tc.psum_pool(name="psum", bufs=BANKS))
+        ctx.enter_context(tc.manual_schedule())
+
+        h_sb = keep.tile([P, TILES, H], BF16)
+        w_words = keep.tile([P, 2 * D], U8, align_bytes=64)
+        w_scales = keep.tile([P, D], U8, align_bytes=64)
+        b3_row = keep.tile([P, D], BF16)
+        b3_bc = keep.tile([P, D], F32)
+        proto_sb = keep.tile([P, D], BF16)
+        ones_bf = keep.tile([P, P], BF16)
+        ident_f = keep.tile([P, P], F32)
+        ident_b = keep.tile([P, P], BF16)
+        half = keep.tile([P, PAIR], F32)
+        minus_one = keep.tile([P, 1], F32)
+        one_col = keep.tile([P, 1], F32)
+        warm = keep.tile([P, 2], F32)
+
+        h_grouped = keep.tile([P, TILES, P, PACK], BF16, align_bytes=64)
+        h_codes = keep.tile([P, TILES, P], U32, align_bytes=64)
+        h_scales = keep.tile([P, TILES, P], U8, align_bytes=64)
+        u_sb = keep.tile([P, TILES, D], F32)
+        hyp_sb = keep.tile([P, TILES, D], F32)
+        hyp_grouped = keep.tile([P, TILES, P, PACK], BF16, align_bytes=64)
+        hyp_codes = keep.tile([P, TILES, P], U32, align_bytes=64)
+        hyp_scales = keep.tile([P, TILES, P], U8, align_bytes=64)
+        proto_grouped = keep.tile([P, N, PACK], BF16, align_bytes=64)
+        proto_codes = keep.tile([P, N], U32, align_bytes=64)
+        proto_scales = keep.tile([P, N], U8, align_bytes=64)
+
+        sumsq = keep.tile([P, TILES], F32)
+        floored = keep.tile([P, TILES], F32)
+        norm = keep.tile([P, TILES], F32)
+        tanh_n = keep.tile([P, TILES], F32)
+        inv_n = keep.tile([P, TILES], F32)
+        shrink = keep.tile([P, TILES], F32)
+        c_shrink2 = keep.tile([P, TILES], F32)
+        minus_cbn = keep.tile([P, TILES], F32)
+        gamma = keep.tile([P, TILES], F32)
+        gamma_inv = keep.tile([P, TILES], F32)
+
+        a_col = keep.tile([P, 1], F32)
+        beta_col = keep.tile([P, 1], F32)
+        beta_floor = keep.tile([P, 1], F32)
+        beta_inv = keep.tile([P, 1], F32)
+        repeated = keep.tile([P, 2, P], F32)
+        proto_rows = keep.tile([P, 2, N], F32)
+
+        ca_plus_cbn = keep.tile([P, TILES, N], F32)
+        c_gap = keep.tile([P, TILES, N], F32)
+        scaled_gap = keep.tile([P, TILES, N], F32)
+        sinh_t = keep.tile([P, TILES, N], F32)
+        cosh_t = keep.tile([P, TILES, N], F32)
+        exp_theta = keep.tile([P, TILES, N], F32)
+        theta = keep.tile([P, TILES, N], F32)
+        logit_sb = keep.tile([P, TILES, N], F32)
+
+        ht_ps = {}
+        u_ps = {}
+        hypt_ps = {}
+        p_ps = {}
+
+        def bank(shape, dtype, name):
+            return psum.tile(shape, dtype, tag="bank", name=name)
+
+        nc.vector.memset(b3_row[:], 0.0)
+        nc.vector.memset(w_scales[:].bitcast(I32), 0)
+        nc.vector.memset(ones_bf[:], 1.0)
+        nc.vector.memset(half[:], 0.5)
+        nc.vector.memset(minus_one[:], -1.0)
+        nc.vector.memset(one_col[:], 1.0)
+        make_identity(nc, ident_f[:])
+        make_identity(nc, ident_b[:])
+
+        nc.sync.dma_start(out=b3_row[0:1, :], in_=b3.rearrange("(o d) -> o d", o=1))
+        nc.sync.dma_start(out=h_sb[:, tiles_of(0), :], in_=h_rows[:, tiles_of(0), :])
+        nc.sync.dma_start(out=proto_sb[:], in_=prototypes)
+        nc.sync.dma_start(out=h_sb[:, tiles_of(1), :], in_=h_rows[:, tiles_of(1), :])
+        nc.sync.dma_start(out=h_sb[:, tiles_of(2), :], in_=h_rows[:, tiles_of(2), :])
+        nc.sync.dma_start(out=w_words[:].bitcast(I32), in_=W3_words[0].bitcast(I32))
+        for quad in range(4):
+            nc.sync.dma_start(
+                out=w_scales[32 * quad : 32 * quad + 4, :].bitcast(I32),
+                in_=W3_scales[0, 4 * quad : 4 * quad + 4, :].bitcast(I32),
+            )
+
+        nc.scalar.activation(out=warm[:, 0:1], in_=half[:, 0:1], func=ACT.Tanh)
+
+        def broadcast_bias():
+            b3_ps = bank([P, D], F32, "b3_ps")
+            nc.tensor.matmul(out=b3_ps[:], lhsT=ones_bf[:], rhs=b3_row[:], start=True, stop=True)
+            nc.scalar.copy(out=b3_bc[:], in_=b3_ps[:])
+
+        def transpose_h(j):
+            ht_ps[j] = bank([P, PAIR, 2, P], F32, "ht_ps")
+            for i in range(PAIR):
+                words = h_sb[:, PAIR * j + i, :].bitcast(F32)
+                for w in range(2):
+                    nc.tensor.transpose(ht_ps[j][:, i, w, :], words[:, w : H // 2 : 2], ident_f[:])
+
+        def copy_h(j):
+            nc.scalar.copy(
+                out=h_grouped[:, tiles_of(j), :, :].bitcast(F32),
+                in_=ht_ps[j][:].rearrange("p i w r -> p i r w"),
+            )
+
+        def quantise_h(j):
+            nc.vector.quantize_mx(
+                out=h_codes[:, tiles_of(j), :].rearrange("p i r -> p (i r)").bitcast(FP8X4),
+                scales=h_scales[:, tiles_of(j), :].rearrange("p i r -> p (i r)"),
+                in_=h_grouped[:, tiles_of(j), :, :].rearrange("p i r t -> p (i r t)"),
+            )
+
+        def first_matmul(j):
+            for t in range(PAIR * j, PAIR * (j + 1)):
+                u_ps[t] = bank([P, D], F32, "u_ps")
+                nc.tensor.matmul_mx(
+                    out=u_ps[t][:],
+                    lhsT=h_codes[:, t, :].bitcast(FP8X4),
+                    lhsT_scale=h_scales[:, t, :],
+                    rhs=w_words[:].bitcast(FP4X4),
+                    rhs_scale=w_scales[:],
+                    start=True,
+                    stop=True,
+                )
+
+        def add_bias(j):
+            for t in range(PAIR * j, PAIR * (j + 1)):
+                nc.vector.tensor_tensor(out=u_sb[:, t, :], in0=u_ps[t][:], in1=b3_bc[:], op=ALU.add)
+
+        def sum_squares(j):
+            for t in range(PAIR * j, PAIR * (j + 1)):
+                squares = scratch.tile([P, D], F32, name="squares")
+                nc.scalar.activation(
+                    out=squares[:], in_=u_sb[:, t, :], func=ACT.Square, accum_out=sumsq[:, t : t + 1]
+                )
+
+        def norm_of_u(j):
+            nc.vector.tensor_scalar_max(
+                out=floored[:, tiles_of(j)], in0=sumsq[:, tiles_of(j)], scalar1=MIN_NORM * MIN_NORM
+            )
+            nc.gpsimd.tensor_tensor(
+                out=norm[:, tiles_of(j)], in0=floored[:, tiles_of(j)], in1=half[:], op=ALU.pow
+            )
+
+        def tanh_of_norm(j):
+            nc.scalar.activation(
+                out=tanh_n[:, tiles_of(j)], in_=norm[:, tiles_of(j)], func=ACT.Tanh, scale=SQRT_C
+            )
+
+        def inverse_norm(j):
+            nc.vector.reciprocal(out=inv_n[:, tiles_of(j)], in_=norm[:, tiles_of(j)])
+
+        def hyp_of_u(j):
+            nc.vector.scalar_tensor_tensor(
+                out=shrink[:, tiles_of(j)],
+                in0=tanh_n[:, tiles_of(j)],
+                scalar=1.0 / SQRT_C,
+                in1=inv_n[:, tiles_of(j)],
+                op0=ALU.mult,
+                op1=ALU.mult,
+            )
+            for t in range(PAIR * j, PAIR * (j + 1)):
+                nc.vector.tensor_scalar_mul(
+                    out=hyp_sb[:, t, :], in0=u_sb[:, t, :], scalar1=shrink[:, t : t + 1]
+                )
+            nc.sync.dma_start(out=hyp_rows[:, tiles_of(j), :], in_=hyp_sb[:, tiles_of(j), :])
+
+        def transpose_hyp(j):
+            for t in range(PAIR * j, PAIR * (j + 1)):
+                hypt_ps[t] = bank([P, PACK, P], F32, "hypt_ps")
+                for q in range(PACK):
+                    nc.tensor.transpose(
+                        hypt_ps[t][:, q, :], hyp_sb[:, t, q * P : (q + 1) * P], ident_f[:]
+                    )
+
+        def copy_hyp(j):
+            for t in range(PAIR * j, PAIR * (j + 1)):
+                nc.scalar.copy(
+                    out=hyp_grouped[:, t, :, :], in_=hypt_ps[t][:].rearrange("p q r -> p r q")
+                )
+
+        def quantise_hyp(j):
+            nc.vector.quantize_mx(
+                out=hyp_codes[:, tiles_of(j), :].rearrange("p i r -> p (i r)").bitcast(FP8X4),
+                scales=hyp_scales[:, tiles_of(j), :].rearrange("p i r -> p (i r)"),
+                in_=hyp_grouped[:, tiles_of(j), :, :].rearrange("p i r t -> p (i r t)"),
+            )
+
+        def second_matmul(j):
+            p_ps[j] = bank([P, PAIR, N], F32, "p_ps")
+            for i in range(PAIR):
+                nc.tensor.matmul_mx(
+                    out=p_ps[j][:, i, :],
+                    lhsT=hyp_codes[:, PAIR * j + i, :].bitcast(FP8X4),
+                    lhsT_scale=hyp_scales[:, PAIR * j + i, :],
+                    rhs=proto_codes[:].bitcast(FP8X4),
+                    rhs_scale=proto_scales[:],
+                    start=True,
+                    stop=True,
+                )
+
+        def prototype_sums():
+            squares = scratch.tile([P, D], F32, name="squares")
+            nc.scalar.activation(out=squares[:], in_=proto_sb[:], func=ACT.Square, accum_out=a_col[:])
+            nc.gpsimd.tensor_scalar(
+                out=beta_col[:], in0=a_col[:], scalar1=-C, scalar2=1.0, op0=ALU.mult, op1=ALU.add
+            )
+            nc.gpsimd.tensor_scalar_max(out=beta_floor[:], in0=beta_col[:], scalar1=BALL_EDGE)
+            nc.gpsimd.tensor_tensor(out=beta_inv[:], in0=beta_floor[:], in1=minus_one[:], op=ALU.pow)
+
+        def transpose_prototypes():
+            protot_ps = bank([P, PACK, N], BF16, "protot_ps")
+            for q in range(PACK):
+                nc.tensor.transpose(protot_ps[:, q, :], proto_sb[:, q * P : (q + 1) * P], ident_b[:])
+            return protot_ps
+
+        def repeat_prototype_sums():
+            nc.vector.tensor_scalar_mul(
+                out=repeated[:, 0, :], in0=a_col[:, 0:1].to_broadcast([P, P]), scalar1=C
+            )
+            nc.vector.tensor_copy(out=repeated[:, 1, :], in_=beta_inv[:, 0:1].to_broadcast([P, P]))
+            rows_ps = bank([P, 2, N], F32, "rows_ps")
+            for v in range(2):
+                nc.tensor.transpose(rows_ps[:, v, :], repeated[:, v, :], ident_f[:])
+            return rows_ps
+
+        def ball_terms():
+            nc.vector.scalar_tensor_tensor(
+                out=c_shrink2[:], in0=shrink[:], scalar=C, in1=shrink[:], op0=ALU.mult, op1=ALU.mult
+            )
+            nc.vector.scalar_tensor_tensor(
+                out=minus_cbn[:], in0=c_shrink2[:], scalar=-1.0, in1=sumsq[:], op0=ALU.mult, op1=ALU.mult
+            )
+            nc.vector.tensor_scalar(
+                out=gamma[:], in0=minus_cbn[:], scalar1=1.0, scalar2=BALL_EDGE, op0=ALU.add, op1=ALU.max
+            )
+            nc.vector.reciprocal(out=gamma_inv[:], in_=gamma[:])
+
+        def sum_of_norms(j):
+            for t in range(PAIR * j, PAIR * (j + 1)):
+                nc.vector.tensor_scalar_sub(
+                    out=ca_plus_cbn[:, t, :], in0=proto_rows[:, 0, :], scalar1=minus_cbn[:, t : t + 1]
+                )
+
+        def gap(j):
+            nc.vector.scalar_tensor_tensor(
+                out=c_gap[:, tiles_of(j), :],
+                in0=p_ps[j][:],
+                scalar=-2.0 * C,
+                in1=ca_plus_cbn[:, tiles_of(j), :],
+                op0=ALU.mult,
+                op1=ALU.add,
+            )
+            nc.vector.scalar_tensor_tensor(
+                out=scaled_gap[:, tiles_of(j), :],
+                in0=c_gap[:, tiles_of(j), :],
+                scalar=MIN_NORM,
+                in1=proto_rows[:, 1, :].unsqueeze(1).to_broadcast([P, PAIR, N]),
+                op0=ALU.max,
+                op1=ALU.mult,
+            )
+
+        def sinh_and_cosh(j):
+            for t in range(PAIR * j, PAIR * (j + 1)):
+                nc.scalar.activation(
+                    out=sinh_t[:, t, :],
+                    in_=scaled_gap[:, t, :],
+                    func=ACT.Sqrt,
+                    scale=gamma_inv[:, t : t + 1],
+                )
+                nc.scalar.activation(
+                    out=cosh_t[:, t, :],
+                    in_=scaled_gap[:, t, :],
+                    func=ACT.Sqrt,
+                    scale=gamma_inv[:, t : t + 1],
+                    bias=one_col[:],
+                )
+
+        def exp_of_theta(j):
+            nc.vector.tensor_tensor(
+                out=exp_theta[:, tiles_of(j), :],
+                in0=sinh_t[:, tiles_of(j), :],
+                in1=cosh_t[:, tiles_of(j), :],
+                op=ALU.add,
+            )
+
+        def logits(j):
+            nc.scalar.activation(
+                out=theta[:, tiles_of(j), :], in_=exp_theta[:, tiles_of(j), :], func=ACT.Ln
+            )
+            nc.vector.tensor_scalar(
+                out=logit_sb[:, tiles_of(j), :],
+                in0=theta[:, tiles_of(j), :],
+                scalar1=LOGIT_SCALE,
+                scalar2=LOGIT_SCALE * ARTANH_MAX,
+                op0=ALU.mult,
+                op1=ALU.max,
+            )
+            nc.sync.dma_start(out=logit_rows[:, tiles_of(j), :], in_=logit_sb[:, tiles_of(j), :])
+
+        broadcast_bias()
+        transpose_h(0)
+        copy_h(0)
+        prototype_sums()
+        transpose_h(1)
+        copy_h(1)
+        quantise_h(0)
+        transpose_h(2)
+        copy_h(2)
+        quantise_h(1)
+        first_matmul(0)
+        first_matmul(1)
+        add_bias(0)
+        quantise_h(2)
+        sum_squares(0)
+        first_matmul(2)
+        add_bias(1)
+        sum_squares(1)
+        norm_of_u(0)
+        add_bias(2)
+        inverse_norm(0)
+        tanh_of_norm(0)
+        sum_squares(2)
+        norm_of_u(1)
+        hyp_of_u(0)
+        inverse_norm(1)
+        tanh_of_norm(1)
+        norm_of_u(2)
+        protot_ps = transpose_prototypes()
+        rows_ps = repeat_prototype_sums()
+        transpose_hyp(0)
+        hyp_of_u(1)
+        nc.vector.tensor_copy(out=proto_grouped[:], in_=protot_ps[:].rearrange("p q n -> p n q"))
+        inverse_norm(2)
+        tanh_of_norm(2)
+        nc.scalar.activation(out=warm[:, 1:2], in_=one_col[:], func=ACT.Sqrt)
+        copy_hyp(0)
+        transpose_hyp(1)
+        hyp_of_u(2)
+        nc.vector.quantize_mx(
+            out=proto_codes[:].bitcast(FP8X4),
+            scales=proto_scales[:],
+            in_=proto_grouped[:].rearrange("p n q -> p (n q)"),
+        )
+        ball_terms()
+        nc.vector.tensor_copy(out=proto_rows[:], in_=rows_ps[:])
+        copy_hyp(1)
+        quantise_hyp(0)
+        for j in range(PAIRS):
+            sum_of_norms(j)
+        transpose_hyp(2)
+        second_matmul(0)
+        copy_hyp(2)
+        quantise_hyp(1)
+        second_matmul(1)
+        gap(0)
+        sinh_and_cosh(0)
+        quantise_hyp(2)
+        second_matmul(2)
+        gap(1)
+        sinh_and_cosh(1)
+        gap(2)
+        sinh_and_cosh(2)
+        for j in range(PAIRS):
+            exp_of_theta(j)
+        for j in range(PAIRS):
+            logits(j)

@@ -121,7 +121,7 @@ def tile_hyperbolicuniform_pa_s_kernel(
         make_identity(nc, ident_f[:])
         make_identity(nc, ident_b[:])
 
-        nc.sync.dma_start(out=b3_row[0:1, :], in_=b3.rearrange("(o d) -> o d", o=1))
+        nc.scalar.dma_start(out=b3_row[0:1, :], in_=b3.rearrange("(o d) -> o d", o=1))
         nc.sync.dma_start(out=h_sb[:, tiles_of(0), :], in_=h_rows[:, tiles_of(0), :])
         nc.sync.dma_start(out=proto_sb[:], in_=prototypes)
         nc.sync.dma_start(out=h_sb[:, tiles_of(1), :], in_=h_rows[:, tiles_of(1), :])
@@ -138,7 +138,7 @@ def tile_hyperbolicuniform_pa_s_kernel(
         def broadcast_bias():
             b3_ps = bank([P, D], F32, "b3_ps")
             nc.tensor.matmul(out=b3_ps[:], lhsT=ones_bf[:], rhs=b3_row[:], start=True, stop=True)
-            nc.scalar.copy(out=b3_bc[:], in_=b3_ps[:])
+            return b3_ps
 
         def transpose_h(j):
             ht_ps[j] = bank([P, PAIR, 2, P], F32, "ht_ps")
@@ -269,6 +269,8 @@ def tile_hyperbolicuniform_pa_s_kernel(
                 out=repeated[:, 0, :], in0=a_col[:, 0:1].to_broadcast([P, P]), scalar1=C
             )
             nc.vector.tensor_copy(out=repeated[:, 1, :], in_=beta_inv[:, 0:1].to_broadcast([P, P]))
+
+        def transpose_prototype_sums():
             rows_ps = bank([P, 2, N], F32, "rows_ps")
             for v in range(2):
                 nc.tensor.transpose(rows_ps[:, v, :], repeated[:, v, :], ident_f[:])
@@ -301,6 +303,8 @@ def tile_hyperbolicuniform_pa_s_kernel(
                 op0=ALU.mult,
                 op1=ALU.add,
             )
+
+        def scale_gap(j):
             nc.vector.scalar_tensor_tensor(
                 out=scaled_gap[:, tiles_of(j), :],
                 in0=c_gap[:, tiles_of(j), :],
@@ -348,12 +352,13 @@ def tile_hyperbolicuniform_pa_s_kernel(
             )
             nc.sync.dma_start(out=logit_rows[:, tiles_of(j), :], in_=logit_sb[:, tiles_of(j), :])
 
-        broadcast_bias()
         transpose_h(0)
-        copy_h(0)
         prototype_sums()
+        copy_h(0)
         transpose_h(1)
         copy_h(1)
+        b3_ps = broadcast_bias()
+        nc.scalar.copy(out=b3_bc[:], in_=b3_ps[:])
         quantise_h(0)
         transpose_h(2)
         copy_h(2)
@@ -368,6 +373,7 @@ def tile_hyperbolicuniform_pa_s_kernel(
         sum_squares(1)
         norm_of_u(0)
         add_bias(2)
+        repeat_prototype_sums()
         inverse_norm(0)
         tanh_of_norm(0)
         sum_squares(2)
@@ -377,13 +383,13 @@ def tile_hyperbolicuniform_pa_s_kernel(
         tanh_of_norm(1)
         norm_of_u(2)
         protot_ps = transpose_prototypes()
-        rows_ps = repeat_prototype_sums()
+        rows_ps = transpose_prototype_sums()
+        nc.scalar.copy(out=proto_grouped[:], in_=protot_ps[:].rearrange("p q n -> p n q"))
+        nc.scalar.copy(out=proto_rows[:], in_=rows_ps[:])
         transpose_hyp(0)
         hyp_of_u(1)
-        nc.vector.tensor_copy(out=proto_grouped[:], in_=protot_ps[:].rearrange("p q n -> p n q"))
         inverse_norm(2)
         tanh_of_norm(2)
-        nc.scalar.activation(out=warm[:, 1:2], in_=one_col[:], func=ACT.Sqrt)
         copy_hyp(0)
         transpose_hyp(1)
         hyp_of_u(2)
@@ -392,26 +398,32 @@ def tile_hyperbolicuniform_pa_s_kernel(
             scales=proto_scales[:],
             in_=proto_grouped[:].rearrange("p n q -> p (n q)"),
         )
-        ball_terms()
-        nc.vector.tensor_copy(out=proto_rows[:], in_=rows_ps[:])
         copy_hyp(1)
-        quantise_hyp(0)
-        for j in range(PAIRS):
-            sum_of_norms(j)
         transpose_hyp(2)
+        quantise_hyp(0)
+        ball_terms()
+        sum_of_norms(0)
         second_matmul(0)
         copy_hyp(2)
+        nc.scalar.activation(out=warm[:, 1:2], in_=one_col[:], func=ACT.Sqrt)
         quantise_hyp(1)
         second_matmul(1)
         gap(0)
+        sum_of_norms(1)
+        scale_gap(0)
         sinh_and_cosh(0)
         quantise_hyp(2)
+        sum_of_norms(2)
         second_matmul(2)
         gap(1)
+        scale_gap(1)
         sinh_and_cosh(1)
         gap(2)
+        scale_gap(2)
         sinh_and_cosh(2)
-        for j in range(PAIRS):
-            exp_of_theta(j)
-        for j in range(PAIRS):
-            logits(j)
+        exp_of_theta(0)
+        exp_of_theta(1)
+        exp_of_theta(2)
+        logits(0)
+        logits(1)
+        logits(2)

@@ -54,15 +54,15 @@ def tile_hyperbolicuniform_pa_s_kernel(
         h_sb = keep.tile([P, TILES, H], BF16)
         w_words = keep.tile([P, 2 * D], U8, align_bytes=64)
         w_scales = keep.tile([P, D], U8, align_bytes=64)
+        warm_ones = keep.tile([P, P], F32)
         b3_row = keep.tile([P, D], BF16)
         b3_bc = keep.tile([P, D], F32)
         proto_sb = keep.tile([P, D], BF16)
         ones_bf = keep.tile([P, P], BF16)
         ident_f = keep.tile([P, P], F32)
-        ident_b = keep.tile([P, P], BF16)
-        half = keep.tile([P, PAIR], F32)
-        minus_one = keep.tile([P, 1], F32)
+        minus_half = keep.tile([P, PAIR], F32)
         one_col = keep.tile([P, 1], F32)
+        u_floor = keep.tile([P, 1], F32)
         warm = keep.tile([P, 2], F32)
 
         h_grouped = keep.tile([P, TILES, P, PACK], BF16, align_bytes=64)
@@ -70,6 +70,7 @@ def tile_hyperbolicuniform_pa_s_kernel(
         h_scales = keep.tile([P, TILES, P], U8, align_bytes=64)
         u_sb = keep.tile([P, TILES, D], F32)
         hyp_sb = keep.tile([P, TILES, D], F32)
+        hyp_bf = keep.tile([P, TILES, D], BF16)
         hyp_grouped = keep.tile([P, TILES, P, PACK], BF16, align_bytes=64)
         hyp_codes = keep.tile([P, TILES, P], U32, align_bytes=64)
         hyp_scales = keep.tile([P, TILES, P], U8, align_bytes=64)
@@ -78,13 +79,10 @@ def tile_hyperbolicuniform_pa_s_kernel(
         proto_scales = keep.tile([P, N], U8, align_bytes=64)
 
         sumsq = keep.tile([P, TILES], F32)
-        floored = keep.tile([P, TILES], F32)
-        norm = keep.tile([P, TILES], F32)
         tanh_n = keep.tile([P, TILES], F32)
-        inv_n = keep.tile([P, TILES], F32)
-        shrink = keep.tile([P, TILES], F32)
-        c_shrink2 = keep.tile([P, TILES], F32)
-        minus_cbn = keep.tile([P, TILES], F32)
+        inv_x = keep.tile([P, TILES], F32)
+        c_bn = keep.tile([P, TILES], F32)
+        gamma_raw = keep.tile([P, TILES], F32)
         gamma = keep.tile([P, TILES], F32)
         gamma_inv = keep.tile([P, TILES], F32)
 
@@ -92,10 +90,9 @@ def tile_hyperbolicuniform_pa_s_kernel(
         beta_col = keep.tile([P, 1], F32)
         beta_floor = keep.tile([P, 1], F32)
         beta_inv = keep.tile([P, 1], F32)
-        repeated = keep.tile([P, 2, P], F32)
         proto_rows = keep.tile([P, 2, N], F32)
 
-        ca_plus_cbn = keep.tile([P, TILES, N], F32)
+        norm_sums = keep.tile([P, TILES, N], F32)
         c_gap = keep.tile([P, TILES, N], F32)
         scaled_gap = keep.tile([P, TILES, N], F32)
         sinh_t = keep.tile([P, TILES, N], F32)
@@ -112,28 +109,37 @@ def tile_hyperbolicuniform_pa_s_kernel(
         def bank(shape, dtype, name):
             return psum.tile(shape, dtype, tag="bank", name=name)
 
-        nc.vector.memset(b3_row[:], 0.0)
-        nc.vector.memset(w_scales[:].bitcast(I32), 0)
+        nc.vector.memset(warm_ones[:], 1.0)
+        nc.vector.memset(minus_half[:], -0.5)
+        nc.vector.memset(b3_row[:].bitcast(I32), 0)
         nc.vector.memset(ones_bf[:], 1.0)
-        nc.vector.memset(half[:], 0.5)
-        nc.vector.memset(minus_one[:], -1.0)
         nc.vector.memset(one_col[:], 1.0)
+        nc.vector.memset(u_floor[:], SQRT_C * MIN_NORM / math.sqrt(D))
         make_identity(nc, ident_f[:])
-        make_identity(nc, ident_b[:])
 
-        nc.scalar.dma_start(out=b3_row[0:1, :], in_=b3.rearrange("(o d) -> o d", o=1))
-        nc.sync.dma_start(out=h_sb[:, tiles_of(0), :], in_=h_rows[:, tiles_of(0), :])
-        nc.sync.dma_start(out=proto_sb[:], in_=prototypes)
-        nc.sync.dma_start(out=h_sb[:, tiles_of(1), :], in_=h_rows[:, tiles_of(1), :])
-        nc.sync.dma_start(out=h_sb[:, tiles_of(2), :], in_=h_rows[:, tiles_of(2), :])
+        nc.scalar.activation(out=warm[:, 0:1], in_=minus_half[:, 0:1], func=ACT.Tanh)
+        nc.gpsimd.dma_start(out=b3_row[0:1, :], in_=b3.rearrange("(o d) -> o d", o=1))
+
+        for j in range(2):
+            nc.sync.dma_start(out=h_sb[:, tiles_of(j), :], in_=h_rows[:, tiles_of(j), :])
         nc.sync.dma_start(out=w_words[:].bitcast(I32), in_=W3_words[0].bitcast(I32))
         for quad in range(4):
             nc.sync.dma_start(
-                out=w_scales[32 * quad : 32 * quad + 4, :].bitcast(I32),
-                in_=W3_scales[0, 4 * quad : 4 * quad + 4, :].bitcast(I32),
+                out=w_scales[32 * quad : 32 * quad + 32, :].bitcast(I32),
+                in_=W3_scales[0, 4 * quad : 4 * quad + 4, :]
+                .bitcast(I32)
+                .unsqueeze(0)
+                .to_broadcast([8, 4, D // 4]),
             )
+        nc.sync.dma_start(out=h_sb[:, tiles_of(2), :], in_=h_rows[:, tiles_of(2), :])
+        nc.sync.dma_start(out=proto_sb[:], in_=prototypes)
 
-        nc.scalar.activation(out=warm[:, 0:1], in_=half[:, 0:1], func=ACT.Tanh)
+        def warm_tensor_engine():
+            for i in range(3):
+                spare_ps = bank([P, P], F32, "spare_ps")
+                nc.tensor.matmul(
+                    out=spare_ps[:], lhsT=warm_ones[:], rhs=warm_ones[:], start=True, stop=True
+                )
 
         def broadcast_bias():
             b3_ps = bank([P, D], F32, "b3_ps")
@@ -141,23 +147,24 @@ def tile_hyperbolicuniform_pa_s_kernel(
             return b3_ps
 
         def transpose_h(j):
-            ht_ps[j] = bank([P, PAIR, 2, P], F32, "ht_ps")
-            for i in range(PAIR):
-                words = h_sb[:, PAIR * j + i, :].bitcast(F32)
+            for t in range(PAIR * j, PAIR * (j + 1)):
+                ht_ps[t] = bank([P, 2, P], F32, "ht_ps")
+                words = h_sb[:, t, :].bitcast(F32)
                 for w in range(2):
-                    nc.tensor.transpose(ht_ps[j][:, i, w, :], words[:, w : H // 2 : 2], ident_f[:])
+                    nc.tensor.transpose(ht_ps[t][:, w, :], words[:, w : H // 2 : 2], ident_f[:])
 
         def copy_h(j):
-            nc.scalar.copy(
-                out=h_grouped[:, tiles_of(j), :, :].bitcast(F32),
-                in_=ht_ps[j][:].rearrange("p i w r -> p i r w"),
-            )
+            for t in range(PAIR * j, PAIR * (j + 1)):
+                nc.scalar.copy(
+                    out=h_grouped[:, t, :, :].bitcast(F32),
+                    in_=ht_ps[t][:].rearrange("p w r -> p r w"),
+                )
 
-        def quantise_h(j):
+        def quantise_h(tiles):
             nc.vector.quantize_mx(
-                out=h_codes[:, tiles_of(j), :].rearrange("p i r -> p (i r)").bitcast(FP8X4),
-                scales=h_scales[:, tiles_of(j), :].rearrange("p i r -> p (i r)"),
-                in_=h_grouped[:, tiles_of(j), :, :].rearrange("p i r t -> p (i r t)"),
+                out=h_codes[:, tiles, :].rearrange("p i r -> p (i r)").bitcast(FP8X4),
+                scales=h_scales[:, tiles, :].rearrange("p i r -> p (i r)"),
+                in_=h_grouped[:, tiles, :, :].rearrange("p i r t -> p (i r t)"),
             )
 
         def first_matmul(j):
@@ -173,60 +180,63 @@ def tile_hyperbolicuniform_pa_s_kernel(
                     stop=True,
                 )
 
-        def add_bias(j):
-            for t in range(PAIR * j, PAIR * (j + 1)):
-                nc.vector.tensor_tensor(out=u_sb[:, t, :], in0=u_ps[t][:], in1=b3_bc[:], op=ALU.add)
+        def add_bias(t):
+            nc.vector.tensor_tensor(out=u_sb[:, t, :], in0=u_ps[t][:], in1=b3_bc[:], op=ALU.add)
 
-        def sum_squares(j):
-            for t in range(PAIR * j, PAIR * (j + 1)):
-                squares = scratch.tile([P, D], F32, name="squares")
-                nc.scalar.activation(
-                    out=squares[:], in_=u_sb[:, t, :], func=ACT.Square, accum_out=sumsq[:, t : t + 1]
-                )
+        def sum_squares(t):
+            squares = scratch.tile([P, D], F32, name="squares")
+            nc.scalar.activation(
+                out=squares[:],
+                in_=u_sb[:, t, :],
+                func=ACT.Square,
+                scale=SQRT_C,
+                bias=u_floor[:],
+                accum_out=sumsq[:, t : t + 1],
+            )
 
         def norm_of_u(j):
-            nc.vector.tensor_scalar_max(
-                out=floored[:, tiles_of(j)], in0=sumsq[:, tiles_of(j)], scalar1=MIN_NORM * MIN_NORM
-            )
             nc.gpsimd.tensor_tensor(
-                out=norm[:, tiles_of(j)], in0=floored[:, tiles_of(j)], in1=half[:], op=ALU.pow
+                out=inv_x[:, tiles_of(j)], in0=sumsq[:, tiles_of(j)], in1=minus_half[:], op=ALU.pow
             )
 
         def tanh_of_norm(j):
-            nc.scalar.activation(
-                out=tanh_n[:, tiles_of(j)], in_=norm[:, tiles_of(j)], func=ACT.Tanh, scale=SQRT_C
-            )
+            for t in range(PAIR * j, PAIR * (j + 1)):
+                nc.scalar.activation(
+                    out=tanh_n[:, t : t + 1],
+                    in_=sumsq[:, t : t + 1],
+                    func=ACT.Tanh,
+                    scale=inv_x[:, t : t + 1],
+                )
 
-        def inverse_norm(j):
-            nc.vector.reciprocal(out=inv_n[:, tiles_of(j)], in_=norm[:, tiles_of(j)])
-
-        def hyp_of_u(j):
-            nc.vector.scalar_tensor_tensor(
-                out=shrink[:, tiles_of(j)],
-                in0=tanh_n[:, tiles_of(j)],
-                scalar=1.0 / SQRT_C,
-                in1=inv_n[:, tiles_of(j)],
+        def hyp_of_tile(t, hyp):
+            nc.vector.tensor_scalar(
+                out=hyp[:, t, :],
+                in0=u_sb[:, t, :],
+                scalar1=tanh_n[:, t : t + 1],
+                scalar2=inv_x[:, t : t + 1],
                 op0=ALU.mult,
                 op1=ALU.mult,
             )
+
+        def hyp_of_u(j, hyp):
             for t in range(PAIR * j, PAIR * (j + 1)):
-                nc.vector.tensor_scalar_mul(
-                    out=hyp_sb[:, t, :], in0=u_sb[:, t, :], scalar1=shrink[:, t : t + 1]
-                )
+                hyp_of_tile(t, hyp)
+
+        def store_hyp(j):
             nc.sync.dma_start(out=hyp_rows[:, tiles_of(j), :], in_=hyp_sb[:, tiles_of(j), :])
 
         def transpose_hyp(j):
             for t in range(PAIR * j, PAIR * (j + 1)):
-                hypt_ps[t] = bank([P, PACK, P], F32, "hypt_ps")
-                for q in range(PACK):
-                    nc.tensor.transpose(
-                        hypt_ps[t][:, q, :], hyp_sb[:, t, q * P : (q + 1) * P], ident_f[:]
-                    )
+                hypt_ps[t] = bank([P, 2, P], F32, "hypt_ps")
+                words = hyp_bf[:, t, :].bitcast(F32)
+                for w in range(2):
+                    nc.tensor.transpose(hypt_ps[t][:, w, :], words[:, w : D // 2 : 2], ident_f[:])
 
-        def copy_hyp(j):
+        def copy_hyp(j, copy):
             for t in range(PAIR * j, PAIR * (j + 1)):
-                nc.scalar.copy(
-                    out=hyp_grouped[:, t, :, :], in_=hypt_ps[t][:].rearrange("p q r -> p r q")
+                copy(
+                    out=hyp_grouped[:, t, :, :].bitcast(F32),
+                    in_=hypt_ps[t][:].rearrange("p w r -> p r w"),
                 )
 
         def quantise_hyp(j):
@@ -256,42 +266,37 @@ def tile_hyperbolicuniform_pa_s_kernel(
                 out=beta_col[:], in0=a_col[:], scalar1=-C, scalar2=1.0, op0=ALU.mult, op1=ALU.add
             )
             nc.gpsimd.tensor_scalar_max(out=beta_floor[:], in0=beta_col[:], scalar1=BALL_EDGE)
-            nc.gpsimd.tensor_tensor(out=beta_inv[:], in0=beta_floor[:], in1=minus_one[:], op=ALU.pow)
 
         def transpose_prototypes():
-            protot_ps = bank([P, PACK, N], BF16, "protot_ps")
-            for q in range(PACK):
-                nc.tensor.transpose(protot_ps[:, q, :], proto_sb[:, q * P : (q + 1) * P], ident_b[:])
+            protot_ps = bank([P, 2, N], F32, "protot_ps")
+            words = proto_sb[:].bitcast(F32)
+            for w in range(2):
+                nc.tensor.transpose(protot_ps[:, w, :], words[:, w : D // 2 : 2], ident_f[:])
             return protot_ps
-
-        def repeat_prototype_sums():
-            nc.vector.tensor_scalar_mul(
-                out=repeated[:, 0, :], in0=a_col[:, 0:1].to_broadcast([P, P]), scalar1=C
-            )
-            nc.vector.tensor_copy(out=repeated[:, 1, :], in_=beta_inv[:, 0:1].to_broadcast([P, P]))
 
         def transpose_prototype_sums():
             rows_ps = bank([P, 2, N], F32, "rows_ps")
-            for v in range(2):
-                nc.tensor.transpose(rows_ps[:, v, :], repeated[:, v, :], ident_f[:])
+            for v, column in enumerate((a_col, beta_inv)):
+                nc.tensor.transpose(
+                    rows_ps[:, v, :], column[:, 0:1].to_broadcast([P, P]), ident_f[:]
+                )
             return rows_ps
 
-        def ball_terms():
-            nc.vector.scalar_tensor_tensor(
-                out=c_shrink2[:], in0=shrink[:], scalar=C, in1=shrink[:], op0=ALU.mult, op1=ALU.mult
+        def gamma_terms():
+            nc.gpsimd.tensor_scalar(
+                out=gamma_raw[:], in0=c_bn[:], scalar1=-1.0, scalar2=1.0, op0=ALU.mult, op1=ALU.add
             )
-            nc.vector.scalar_tensor_tensor(
-                out=minus_cbn[:], in0=c_shrink2[:], scalar=-1.0, in1=sumsq[:], op0=ALU.mult, op1=ALU.mult
-            )
-            nc.vector.tensor_scalar(
-                out=gamma[:], in0=minus_cbn[:], scalar1=1.0, scalar2=BALL_EDGE, op0=ALU.add, op1=ALU.max
-            )
-            nc.vector.reciprocal(out=gamma_inv[:], in_=gamma[:])
+            nc.gpsimd.tensor_scalar_max(out=gamma[:], in0=gamma_raw[:], scalar1=BALL_EDGE)
 
-        def sum_of_norms(j):
+        def sums_of_norms(j):
             for t in range(PAIR * j, PAIR * (j + 1)):
-                nc.vector.tensor_scalar_sub(
-                    out=ca_plus_cbn[:, t, :], in0=proto_rows[:, 0, :], scalar1=minus_cbn[:, t : t + 1]
+                nc.gpsimd.tensor_scalar(
+                    out=norm_sums[:, t, :],
+                    in0=proto_rows[:, 0, :],
+                    scalar1=C,
+                    scalar2=c_bn[:, t : t + 1],
+                    op0=ALU.mult,
+                    op1=ALU.add,
                 )
 
         def gap(j):
@@ -299,7 +304,7 @@ def tile_hyperbolicuniform_pa_s_kernel(
                 out=c_gap[:, tiles_of(j), :],
                 in0=p_ps[j][:],
                 scalar=-2.0 * C,
-                in1=ca_plus_cbn[:, tiles_of(j), :],
+                in1=norm_sums[:, tiles_of(j), :],
                 op0=ALU.mult,
                 op1=ALU.add,
             )
@@ -352,76 +357,93 @@ def tile_hyperbolicuniform_pa_s_kernel(
             )
             nc.sync.dma_start(out=logit_rows[:, tiles_of(j), :], in_=logit_sb[:, tiles_of(j), :])
 
+        warm_tensor_engine()
         transpose_h(0)
-        prototype_sums()
-        copy_h(0)
-        transpose_h(1)
-        copy_h(1)
         b3_ps = broadcast_bias()
-        nc.scalar.copy(out=b3_bc[:], in_=b3_ps[:])
-        quantise_h(0)
-        transpose_h(2)
-        copy_h(2)
-        quantise_h(1)
+        copy_h(0)
+        quantise_h(slice(0, 1))
+        quantise_h(slice(1, 2))
+        transpose_h(1)
+        nc.vector.tensor_copy(out=b3_bc[:], in_=b3_ps[:])
         first_matmul(0)
-        first_matmul(1)
-        add_bias(0)
-        quantise_h(2)
-        sum_squares(0)
-        first_matmul(2)
-        add_bias(1)
-        sum_squares(1)
-        norm_of_u(0)
-        add_bias(2)
-        repeat_prototype_sums()
-        inverse_norm(0)
-        tanh_of_norm(0)
-        sum_squares(2)
-        norm_of_u(1)
-        hyp_of_u(0)
-        inverse_norm(1)
-        tanh_of_norm(1)
-        norm_of_u(2)
+        copy_h(1)
+        transpose_h(2)
         protot_ps = transpose_prototypes()
+        add_bias(0)
+        quantise_h(tiles_of(1))
+        copy_h(2)
+        prototype_sums()
+        add_bias(1)
+        first_matmul(1)
+        quantise_h(tiles_of(2))
+        sum_squares(0)
+        add_bias(2)
+        first_matmul(2)
+        sum_squares(1)
+        add_bias(3)
+        norm_of_u(0)
+        sum_squares(2)
+        add_bias(4)
+        sum_squares(3)
+        add_bias(5)
+        norm_of_u(1)
+        tanh_of_norm(0)
+        nc.vector.reciprocal(out=beta_inv[:], in_=beta_floor[:])
         rows_ps = transpose_prototype_sums()
-        nc.scalar.copy(out=proto_grouped[:], in_=protot_ps[:].rearrange("p q n -> p n q"))
-        nc.scalar.copy(out=proto_rows[:], in_=rows_ps[:])
-        transpose_hyp(0)
-        hyp_of_u(1)
-        inverse_norm(2)
-        tanh_of_norm(2)
-        copy_hyp(0)
-        transpose_hyp(1)
-        hyp_of_u(2)
+        sum_squares(4)
+        nc.vector.tensor_copy(
+            out=proto_grouped[:].bitcast(F32), in_=protot_ps[:].rearrange("p w n -> p n w")
+        )
+        sum_squares(5)
+        hyp_of_u(0, hyp_bf)
+        tanh_of_norm(1)
         nc.vector.quantize_mx(
             out=proto_codes[:].bitcast(FP8X4),
             scales=proto_scales[:],
             in_=proto_grouped[:].rearrange("p n q -> p (n q)"),
         )
-        copy_hyp(1)
-        transpose_hyp(2)
-        quantise_hyp(0)
-        ball_terms()
-        sum_of_norms(0)
-        second_matmul(0)
-        copy_hyp(2)
+        hyp_of_u(1, hyp_bf)
+        norm_of_u(2)
+        nc.scalar.copy(out=proto_rows[:], in_=rows_ps[:])
+        transpose_hyp(0)
+        transpose_hyp(1)
+        copy_hyp(0, nc.scalar.copy)
+        tanh_of_norm(2)
+        nc.scalar.activation(out=c_bn[:], in_=tanh_n[:], func=ACT.Square)
         nc.scalar.activation(out=warm[:, 1:2], in_=one_col[:], func=ACT.Sqrt)
+        hyp_of_tile(0, hyp_sb)
+        quantise_hyp(0)
+        second_matmul(0)
+        hyp_of_u(2, hyp_bf)
+        copy_hyp(1, nc.vector.tensor_copy)
+        transpose_hyp(2)
+        sums_of_norms(0)
+        gamma_terms()
+        sums_of_norms(1)
+        sums_of_norms(2)
         quantise_hyp(1)
-        second_matmul(1)
         gap(0)
-        sum_of_norms(1)
+        copy_hyp(2, nc.scalar.copy)
+        second_matmul(1)
+        nc.vector.reciprocal(out=gamma_inv[:], in_=gamma[:])
         scale_gap(0)
-        sinh_and_cosh(0)
         quantise_hyp(2)
-        sum_of_norms(2)
         second_matmul(2)
         gap(1)
+        sinh_and_cosh(0)
+        hyp_of_tile(1, hyp_sb)
+        store_hyp(0)
         scale_gap(1)
-        sinh_and_cosh(1)
         gap(2)
+        sinh_and_cosh(1)
+        hyp_of_tile(2, hyp_sb)
         scale_gap(2)
         sinh_and_cosh(2)
+        hyp_of_tile(3, hyp_sb)
+        store_hyp(1)
         exp_of_theta(0)
+        hyp_of_u(2, hyp_sb)
+        store_hyp(2)
         exp_of_theta(1)
         exp_of_theta(2)
         logits(0)

@@ -109,16 +109,16 @@ def tile_hyperbolicuniform_pa_s_kernel(
         def bank(shape, dtype, name):
             return psum.tile(shape, dtype, tag="bank", name=name)
 
+        nc.vector.memset(b3_row[:].bitcast(I32), 0)
         nc.vector.memset(warm_ones[:], 1.0)
         nc.vector.memset(minus_half[:], -0.5)
-        nc.vector.memset(b3_row[:].bitcast(I32), 0)
         nc.vector.memset(ones_bf[:], 1.0)
         nc.vector.memset(one_col[:], 1.0)
         nc.vector.memset(u_floor[:], SQRT_C * MIN_NORM / math.sqrt(D))
         make_identity(nc, ident_f[:])
 
+        nc.scalar.dma_start(out=b3_row[0:1, :], in_=b3.rearrange("(o d) -> o d", o=1))
         nc.scalar.activation(out=warm[:, 0:1], in_=minus_half[:, 0:1], func=ACT.Tanh)
-        nc.gpsimd.dma_start(out=b3_row[0:1, :], in_=b3.rearrange("(o d) -> o d", o=1))
 
         for j in range(2):
             nc.sync.dma_start(out=h_sb[:, tiles_of(j), :], in_=h_rows[:, tiles_of(j), :])

@@ -81,6 +81,7 @@ def tile_hyperbolicuniform_pa_s_kernel(
         sumsq = keep.tile([P, TILES], F32)
         tanh_n = keep.tile([P, TILES], F32)
         inv_x = keep.tile([P, TILES], F32)
+        shrink = keep.tile([P, 1], F32)
         c_bn = keep.tile([P, TILES], F32)
         gamma_raw = keep.tile([P, TILES], F32)
         gamma = keep.tile([P, TILES], F32)
@@ -282,15 +283,21 @@ def tile_hyperbolicuniform_pa_s_kernel(
                 )
             return rows_ps
 
+        def ball_norms(tiles):
+            nc.scalar.activation(out=c_bn[:, tiles], in_=tanh_n[:, tiles], func=ACT.Square)
+
         def gamma_terms():
             nc.gpsimd.tensor_scalar(
                 out=gamma_raw[:], in0=c_bn[:], scalar1=-1.0, scalar2=1.0, op0=ALU.mult, op1=ALU.add
             )
             nc.gpsimd.tensor_scalar_max(out=gamma[:], in0=gamma_raw[:], scalar1=BALL_EDGE)
+            nc.gpsimd.tensor_tensor(
+                out=shrink[:, 0:1], in0=tanh_n[:, 0:1], in1=inv_x[:, 0:1], op=ALU.mult
+            )
 
         def sums_of_norms(j):
             for t in range(PAIR * j, PAIR * (j + 1)):
-                nc.gpsimd.tensor_scalar(
+                nc.vector.tensor_scalar(
                     out=norm_sums[:, t, :],
                     in0=proto_rows[:, 0, :],
                     scalar1=C,
@@ -397,6 +404,7 @@ def tile_hyperbolicuniform_pa_s_kernel(
         sum_squares(5)
         hyp_of_u(0, hyp_bf)
         tanh_of_norm(1)
+        ball_norms(slice(0, 2 * PAIR))
         nc.vector.quantize_mx(
             out=proto_codes[:].bitcast(FP8X4),
             scales=proto_scales[:],
@@ -409,21 +417,23 @@ def tile_hyperbolicuniform_pa_s_kernel(
         transpose_hyp(1)
         copy_hyp(0, nc.scalar.copy)
         tanh_of_norm(2)
-        nc.scalar.activation(out=c_bn[:], in_=tanh_n[:], func=ACT.Square)
+        ball_norms(tiles_of(2))
         nc.scalar.activation(out=warm[:, 1:2], in_=one_col[:], func=ACT.Sqrt)
-        hyp_of_tile(0, hyp_sb)
+        sums_of_norms(0)
+        sums_of_norms(1)
         quantise_hyp(0)
         second_matmul(0)
         hyp_of_u(2, hyp_bf)
         copy_hyp(1, nc.vector.tensor_copy)
         transpose_hyp(2)
-        sums_of_norms(0)
         gamma_terms()
-        sums_of_norms(1)
         sums_of_norms(2)
         quantise_hyp(1)
         gap(0)
         copy_hyp(2, nc.scalar.copy)
+        nc.scalar.activation(
+            out=hyp_sb[:, 0, :], in_=u_sb[:, 0, :], func=ACT.Copy, scale=shrink[:, 0:1]
+        )
         second_matmul(1)
         nc.vector.reciprocal(out=gamma_inv[:], in_=gamma[:])
         scale_gap(0)

@@ -121,8 +121,8 @@ def tile_hyperbolicuniform_pa_s_kernel(
         nc.scalar.dma_start(out=b3_row[0:1, :], in_=b3.rearrange("(o d) -> o d", o=1))
         nc.scalar.activation(out=warm[:, 0:1], in_=minus_half[:, 0:1], func=ACT.Tanh)
 
-        for j in range(2):
-            nc.sync.dma_start(out=h_sb[:, tiles_of(j), :], in_=h_rows[:, tiles_of(j), :])
+        nc.sync.dma_start(out=h_sb[:, :PAIR, :], in_=h_rows[:, :PAIR, :])
+        nc.sync.dma_start(out=h_sb[:, PAIR:, :], in_=h_rows[:, PAIR:, :])
         nc.sync.dma_start(out=w_words[:].bitcast(I32), in_=W3_words[0].bitcast(I32))
         for quad in range(4):
             nc.sync.dma_start(
@@ -132,7 +132,6 @@ def tile_hyperbolicuniform_pa_s_kernel(
                 .unsqueeze(0)
                 .to_broadcast([8, 4, D // 4]),
             )
-        nc.sync.dma_start(out=h_sb[:, tiles_of(2), :], in_=h_rows[:, tiles_of(2), :])
         nc.sync.dma_start(out=proto_sb[:], in_=prototypes)
 
         def warm_tensor_engine():
@@ -168,18 +167,17 @@ def tile_hyperbolicuniform_pa_s_kernel(
                 in_=h_grouped[:, tiles, :, :].rearrange("p i r t -> p (i r t)"),
             )
 
-        def first_matmul(j):
-            for t in range(PAIR * j, PAIR * (j + 1)):
-                u_ps[t] = bank([P, D], F32, "u_ps")
-                nc.tensor.matmul_mx(
-                    out=u_ps[t][:],
-                    lhsT=h_codes[:, t, :].bitcast(FP8X4),
-                    lhsT_scale=h_scales[:, t, :],
-                    rhs=w_words[:].bitcast(FP4X4),
-                    rhs_scale=w_scales[:],
-                    start=True,
-                    stop=True,
-                )
+        def first_matmul(t):
+            u_ps[t] = bank([P, D], F32, "u_ps")
+            nc.tensor.matmul_mx(
+                out=u_ps[t][:],
+                lhsT=h_codes[:, t, :].bitcast(FP8X4),
+                lhsT_scale=h_scales[:, t, :],
+                rhs=w_words[:].bitcast(FP4X4),
+                rhs_scale=w_scales[:],
+                start=True,
+                stop=True,
+            )
 
         def add_bias(t):
             nc.vector.tensor_tensor(out=u_sb[:, t, :], in0=u_ps[t][:], in1=b3_bc[:], op=ALU.add)
@@ -233,12 +231,11 @@ def tile_hyperbolicuniform_pa_s_kernel(
                 for w in range(2):
                     nc.tensor.transpose(hypt_ps[t][:, w, :], words[:, w : D // 2 : 2], ident_f[:])
 
-        def copy_hyp(j, copy):
-            for t in range(PAIR * j, PAIR * (j + 1)):
-                copy(
-                    out=hyp_grouped[:, t, :, :].bitcast(F32),
-                    in_=hypt_ps[t][:].rearrange("p w r -> p r w"),
-                )
+        def copy_hyp(t, copy):
+            copy(
+                out=hyp_grouped[:, t, :, :].bitcast(F32),
+                in_=hypt_ps[t][:].rearrange("p w r -> p r w"),
+            )
 
         def quantise_hyp(j):
             nc.vector.quantize_mx(
@@ -371,21 +368,24 @@ def tile_hyperbolicuniform_pa_s_kernel(
         quantise_h(slice(0, 1))
         quantise_h(slice(1, 2))
         transpose_h(1)
-        nc.vector.tensor_copy(out=b3_bc[:], in_=b3_ps[:])
+        nc.scalar.copy(out=b3_bc[:], in_=b3_ps[:])
         first_matmul(0)
         copy_h(1)
         transpose_h(2)
+        first_matmul(1)
         protot_ps = transpose_prototypes()
         add_bias(0)
         quantise_h(tiles_of(1))
         copy_h(2)
         prototype_sums()
         add_bias(1)
-        first_matmul(1)
+        first_matmul(2)
+        first_matmul(3)
         quantise_h(tiles_of(2))
         sum_squares(0)
         add_bias(2)
-        first_matmul(2)
+        first_matmul(4)
+        first_matmul(5)
         sum_squares(1)
         add_bias(3)
         norm_of_u(0)
@@ -417,6 +417,9 @@ def tile_hyperbolicuniform_pa_s_kernel(
         transpose_hyp(1)
         copy_hyp(0, nc.scalar.copy)
         tanh_of_norm(2)
+        copy_hyp(1, nc.scalar.copy)
+        copy_hyp(2, nc.scalar.copy)
+        copy_hyp(3, nc.scalar.copy)
         ball_norms(tiles_of(2))
         nc.scalar.activation(out=warm[:, 1:2], in_=one_col[:], func=ACT.Sqrt)
         sums_of_norms(0)
@@ -424,13 +427,13 @@ def tile_hyperbolicuniform_pa_s_kernel(
         quantise_hyp(0)
         second_matmul(0)
         hyp_of_u(2, hyp_bf)
-        copy_hyp(1, nc.vector.tensor_copy)
         transpose_hyp(2)
         gamma_terms()
         sums_of_norms(2)
         quantise_hyp(1)
         gap(0)
-        copy_hyp(2, nc.scalar.copy)
+        copy_hyp(4, nc.vector.tensor_copy)
+        copy_hyp(5, nc.vector.tensor_copy)
         nc.scalar.activation(
             out=hyp_sb[:, 0, :], in_=u_sb[:, 0, :], func=ACT.Copy, scale=shrink[:, 0:1]
         )

@@ -121,8 +121,8 @@ def tile_hyperbolicuniform_pa_s_kernel(
         nc.scalar.dma_start(out=b3_row[0:1, :], in_=b3.rearrange("(o d) -> o d", o=1))
         nc.scalar.activation(out=warm[:, 0:1], in_=minus_half[:, 0:1], func=ACT.Tanh)
 
-        nc.sync.dma_start(out=h_sb[:, :PAIR, :], in_=h_rows[:, :PAIR, :])
-        nc.sync.dma_start(out=h_sb[:, PAIR:, :], in_=h_rows[:, PAIR:, :])
+        for j in range(2):
+            nc.sync.dma_start(out=h_sb[:, tiles_of(j), :], in_=h_rows[:, tiles_of(j), :])
         nc.sync.dma_start(out=w_words[:].bitcast(I32), in_=W3_words[0].bitcast(I32))
         for quad in range(4):
             nc.sync.dma_start(
@@ -132,6 +132,7 @@ def tile_hyperbolicuniform_pa_s_kernel(
                 .unsqueeze(0)
                 .to_broadcast([8, 4, D // 4]),
             )
+        nc.sync.dma_start(out=h_sb[:, tiles_of(2), :], in_=h_rows[:, tiles_of(2), :])
         nc.sync.dma_start(out=proto_sb[:], in_=prototypes)
 
         def warm_tensor_engine():
@@ -260,10 +261,11 @@ def tile_hyperbolicuniform_pa_s_kernel(
         def prototype_sums():
             squares = scratch.tile([P, D], F32, name="squares")
             nc.scalar.activation(out=squares[:], in_=proto_sb[:], func=ACT.Square, accum_out=a_col[:])
-            nc.gpsimd.tensor_scalar(
-                out=beta_col[:], in0=a_col[:], scalar1=-C, scalar2=1.0, op0=ALU.mult, op1=ALU.add
+
+        def prototype_betas():
+            nc.scalar.activation(
+                out=beta_col[:], in_=a_col[:], func=ACT.Identity, scale=-C, bias=one_col[:]
             )
-            nc.gpsimd.tensor_scalar_max(out=beta_floor[:], in0=beta_col[:], scalar1=BALL_EDGE)
 
         def transpose_prototypes():
             protot_ps = bank([P, 2, N], F32, "protot_ps")
@@ -284,12 +286,8 @@ def tile_hyperbolicuniform_pa_s_kernel(
             nc.scalar.activation(out=c_bn[:, tiles], in_=tanh_n[:, tiles], func=ACT.Square)
 
         def gamma_terms():
-            nc.gpsimd.tensor_scalar(
-                out=gamma_raw[:], in0=c_bn[:], scalar1=-1.0, scalar2=1.0, op0=ALU.mult, op1=ALU.add
-            )
-            nc.gpsimd.tensor_scalar_max(out=gamma[:], in0=gamma_raw[:], scalar1=BALL_EDGE)
-            nc.gpsimd.tensor_tensor(
-                out=shrink[:, 0:1], in0=tanh_n[:, 0:1], in1=inv_x[:, 0:1], op=ALU.mult
+            nc.scalar.activation(
+                out=gamma_raw[:], in_=c_bn[:], func=ACT.Identity, scale=-1.0, bias=one_col[:]
             )
 
         def sums_of_norms(j):
@@ -383,6 +381,7 @@ def tile_hyperbolicuniform_pa_s_kernel(
         first_matmul(3)
         quantise_h(tiles_of(2))
         sum_squares(0)
+        prototype_betas()
         add_bias(2)
         first_matmul(4)
         first_matmul(5)
@@ -395,12 +394,13 @@ def tile_hyperbolicuniform_pa_s_kernel(
         add_bias(5)
         norm_of_u(1)
         tanh_of_norm(0)
-        nc.vector.reciprocal(out=beta_inv[:], in_=beta_floor[:])
-        rows_ps = transpose_prototype_sums()
+        nc.vector.tensor_scalar_max(out=beta_floor[:], in0=beta_col[:], scalar1=BALL_EDGE)
         sum_squares(4)
         nc.vector.tensor_copy(
             out=proto_grouped[:].bitcast(F32), in_=protot_ps[:].rearrange("p w n -> p n w")
         )
+        nc.vector.reciprocal(out=beta_inv[:], in_=beta_floor[:])
+        rows_ps = transpose_prototype_sums()
         sum_squares(5)
         hyp_of_u(0, hyp_bf)
         tanh_of_norm(1)
@@ -418,9 +418,13 @@ def tile_hyperbolicuniform_pa_s_kernel(
         copy_hyp(0, nc.scalar.copy)
         tanh_of_norm(2)
         copy_hyp(1, nc.scalar.copy)
+        ball_norms(tiles_of(2))
+        nc.scalar.activation(
+            out=shrink[:], in_=tanh_n[:, 0:1], func=ACT.Copy, scale=inv_x[:, 0:1]
+        )
         copy_hyp(2, nc.scalar.copy)
         copy_hyp(3, nc.scalar.copy)
-        ball_norms(tiles_of(2))
+        gamma_terms()
         nc.scalar.activation(out=warm[:, 1:2], in_=one_col[:], func=ACT.Sqrt)
         sums_of_norms(0)
         sums_of_norms(1)
@@ -428,9 +432,9 @@ def tile_hyperbolicuniform_pa_s_kernel(
         second_matmul(0)
         hyp_of_u(2, hyp_bf)
         transpose_hyp(2)
-        gamma_terms()
         sums_of_norms(2)
         quantise_hyp(1)
+        nc.vector.tensor_scalar_max(out=gamma[:], in0=gamma_raw[:], scalar1=BALL_EDGE)
         gap(0)
         copy_hyp(4, nc.vector.tensor_copy)
         copy_hyp(5, nc.vector.tensor_copy)

@@ -110,7 +110,7 @@ def tile_hyperbolicuniform_pa_s_kernel(
         def bank(shape, dtype, name):
             return psum.tile(shape, dtype, tag="bank", name=name)
 
-        nc.vector.memset(b3_row[:].bitcast(I32), 0)
+        nc.gpsimd.memset(b3_row[:].bitcast(I32), 0)
         nc.vector.memset(warm_ones[:], 1.0)
         nc.vector.memset(minus_half[:], -0.5)
         nc.vector.memset(ones_bf[:], 1.0)
@@ -118,11 +118,11 @@ def tile_hyperbolicuniform_pa_s_kernel(
         nc.vector.memset(u_floor[:], SQRT_C * MIN_NORM / math.sqrt(D))
         make_identity(nc, ident_f[:])
 
-        nc.scalar.dma_start(out=b3_row[0:1, :], in_=b3.rearrange("(o d) -> o d", o=1))
         nc.scalar.activation(out=warm[:, 0:1], in_=minus_half[:, 0:1], func=ACT.Tanh)
 
-        for j in range(2):
-            nc.sync.dma_start(out=h_sb[:, tiles_of(j), :], in_=h_rows[:, tiles_of(j), :])
+        nc.sync.dma_start(out=h_sb[:, tiles_of(0), :], in_=h_rows[:, tiles_of(0), :])
+        nc.sync.dma_start(out=b3_row[0:1, :], in_=b3.rearrange("(o d) -> o d", o=1))
+        nc.sync.dma_start(out=h_sb[:, tiles_of(1), :], in_=h_rows[:, tiles_of(1), :])
         nc.sync.dma_start(out=w_words[:].bitcast(I32), in_=W3_words[0].bitcast(I32))
         for quad in range(4):
             nc.sync.dma_start(
@@ -230,7 +230,9 @@ def tile_hyperbolicuniform_pa_s_kernel(
                 hypt_ps[t] = bank([P, 2, P], F32, "hypt_ps")
                 words = hyp_bf[:, t, :].bitcast(F32)
                 for w in range(2):
-                    nc.tensor.transpose(hypt_ps[t][:, w, :], words[:, w : D // 2 : 2], ident_f[:])
+                    nc.tensor.transpose(
+                        hypt_ps[t][:, w, :], words[:, w * P : (w + 1) * P], ident_f[:]
+                    )
 
         def copy_hyp(t, copy):
             copy(
@@ -271,7 +273,7 @@ def tile_hyperbolicuniform_pa_s_kernel(
             protot_ps = bank([P, 2, N], F32, "protot_ps")
             words = proto_sb[:].bitcast(F32)
             for w in range(2):
-                nc.tensor.transpose(protot_ps[:, w, :], words[:, w : D // 2 : 2], ident_f[:])
+                nc.tensor.transpose(protot_ps[:, w, :], words[:, w * P : (w + 1) * P], ident_f[:])
             return protot_ps
 
         def transpose_prototype_sums():

@@ -135,8 +135,8 @@ def tile_hyperbolicuniform_pa_s_kernel(
         nc.sync.dma_start(out=h_sb[:, tiles_of(2), :], in_=h_rows[:, tiles_of(2), :])
         nc.sync.dma_start(out=proto_sb[:], in_=prototypes)
 
-        def warm_tensor_engine():
-            for i in range(3):
+        def warm_tensor_engine(count):
+            for i in range(count):
                 spare_ps = bank([P, P], F32, "spare_ps")
                 nc.tensor.matmul(
                     out=spare_ps[:], lhsT=warm_ones[:], rhs=warm_ones[:], start=True, stop=True
@@ -361,9 +361,10 @@ def tile_hyperbolicuniform_pa_s_kernel(
             )
             nc.sync.dma_start(out=logit_rows[:, tiles_of(j), :], in_=logit_sb[:, tiles_of(j), :])
 
-        warm_tensor_engine()
+        warm_tensor_engine(3)
         transpose_h(0)
         b3_ps = broadcast_bias()
+        warm_tensor_engine(1)
         copy_h(0)
         quantise_h(slice(0, 1))
         quantise_h(slice(1, 2))
@@ -387,6 +388,7 @@ def tile_hyperbolicuniform_pa_s_kernel(
         add_bias(2)
         first_matmul(4)
         first_matmul(5)
+        warm_tensor_engine(2)
         sum_squares(1)
         add_bias(3)
         norm_of_u(0)

import math
from contextlib import ExitStack

import concourse.mybir as mybir
from concourse.masks import make_identity

F32 = mybir.dt.float32
BF16 = mybir.dt.bfloat16
I32 = mybir.dt.int32
U32 = mybir.dt.uint32
U8 = mybir.dt.uint8
FP8X4 = mybir.dt.float8_e4m3fn_x4
FP4X4 = mybir.dt.float4_e2m1fn_x4
ALU = mybir.AluOpType
ACT = mybir.ActivationFunctionType

P = 128
PACK = 4
B, H, D, N = 768, 512, 512, 128
TILES = B // P
PAIR = 2
PAIRS = TILES // PAIR
BANKS = 8

C = 3.0
SQRT_C = math.sqrt(C)
MIN_NORM = 1e-15
EPS = 1e-5
TEMP = 0.07
BALL_EDGE = 1e-9
LOGIT_SCALE = -2.0 / (SQRT_C * TEMP)
ARTANH_MAX = 0.5 * math.log((2.0 - EPS) / EPS)

FLOPS = 2 * B * H * D + 2 * B * D * N


def tile_hyperbolicuniform_pa_s_kernel(
    tc, h_mlp, W3_words, W3_scales, b3, prototypes, out_0, out_1
):
    nc = tc.nc
    h_rows = h_mlp.rearrange("(p t) k -> p t k", t=TILES)
    logit_rows = out_0.rearrange("(p t) n -> p t n", t=TILES)
    hyp_rows = out_1.rearrange("(p t) d -> p t d", t=TILES)

    def tiles_of(j):
        return slice(PAIR * j, PAIR * (j + 1))

    with ExitStack() as ctx:
        keep = ctx.enter_context(tc.tile_pool(name="keep", bufs=1))
        scratch = ctx.enter_context(tc.tile_pool(name="scratch", bufs=4))
        psum = ctx.enter_context(tc.psum_pool(name="psum", bufs=BANKS))
        ctx.enter_context(tc.manual_schedule())

        h_sb = keep.tile([P, TILES, H], BF16)
        w_words = keep.tile([P, 2 * D], U8, align_bytes=64)
        w_scales = keep.tile([P, D], U8, align_bytes=64)
        warm_ones = keep.tile([P, P], F32)
        b3_row = keep.tile([P, D], BF16)
        b3_bc = keep.tile([P, D], F32)
        proto_sb = keep.tile([P, D], BF16)
        ones_bf = keep.tile([P, P], BF16)
        ident_f = keep.tile([P, P], F32)
        minus_half = keep.tile([P, PAIR], F32)
        one_col = keep.tile([P, 1], F32)
        u_floor = keep.tile([P, 1], F32)
        warm = keep.tile([P, 2], F32)

        h_grouped = keep.tile([P, TILES, P, PACK], BF16, align_bytes=64)
        h_codes = keep.tile([P, TILES, P], U32, align_bytes=64)
        h_scales = keep.tile([P, TILES, P], U8, align_bytes=64)
        u_sb = keep.tile([P, TILES, D], F32)
        hyp_sb = keep.tile([P, TILES, D], F32)
        hyp_bf = keep.tile([P, TILES, D], BF16)
        hyp_grouped = keep.tile([P, TILES, P, PACK], BF16, align_bytes=64)
        hyp_codes = keep.tile([P, TILES, P], U32, align_bytes=64)
        hyp_scales = keep.tile([P, TILES, P], U8, align_bytes=64)
        proto_grouped = keep.tile([P, N, PACK], BF16, align_bytes=64)
        proto_codes = keep.tile([P, N], U32, align_bytes=64)
        proto_scales = keep.tile([P, N], U8, align_bytes=64)

        sumsq = keep.tile([P, TILES], F32)
        tanh_n = keep.tile([P, TILES], F32)
        inv_x = keep.tile([P, TILES], F32)
        shrink = keep.tile([P, 1], F32)
        c_bn = keep.tile([P, TILES], F32)
        gamma_raw = keep.tile([P, TILES], F32)
        gamma = keep.tile([P, TILES], F32)
        gamma_inv = keep.tile([P, TILES], F32)

        a_col = keep.tile([P, 1], F32)
        beta_col = keep.tile([P, 1], F32)
        beta_floor = keep.tile([P, 1], F32)
        beta_inv = keep.tile([P, 1], F32)
        proto_rows = keep.tile([P, 2, N], F32)

        norm_sums = keep.tile([P, TILES, N], F32)
        c_gap = keep.tile([P, TILES, N], F32)
        scaled_gap = keep.tile([P, TILES, N], F32)
        sinh_t = keep.tile([P, TILES, N], F32)
        cosh_t = keep.tile([P, TILES, N], F32)
        exp_theta = keep.tile([P, TILES, N], F32)
        theta = keep.tile([P, TILES, N], F32)
        logit_sb = keep.tile([P, TILES, N], F32)

        ht_ps = {}
        u_ps = {}
        hypt_ps = {}
        p_ps = {}

        def bank(shape, dtype, name):
            return psum.tile(shape, dtype, tag="bank", name=name)

        nc.gpsimd.memset(b3_row[:].bitcast(I32), 0)
        nc.vector.memset(warm_ones[:], 1.0)
        nc.vector.memset(minus_half[:], -0.5)
        nc.vector.memset(ones_bf[:], 1.0)
        nc.vector.memset(one_col[:], 1.0)
        nc.vector.memset(u_floor[:], SQRT_C * MIN_NORM / math.sqrt(D))
        make_identity(nc, ident_f[:])

        nc.scalar.activation(out=warm[:, 0:1], in_=minus_half[:, 0:1], func=ACT.Tanh)

        nc.sync.dma_start(out=h_sb[:, tiles_of(0), :], in_=h_rows[:, tiles_of(0), :])
        nc.sync.dma_start(out=b3_row[0:1, :], in_=b3.rearrange("(o d) -> o d", o=1))
        nc.sync.dma_start(out=h_sb[:, tiles_of(1), :], in_=h_rows[:, tiles_of(1), :])
        nc.sync.dma_start(out=w_words[:].bitcast(I32), in_=W3_words[0].bitcast(I32))
        for quad in range(4):
            nc.sync.dma_start(
                out=w_scales[32 * quad : 32 * quad + 32, :].bitcast(I32),
                in_=W3_scales[0, 4 * quad : 4 * quad + 4, :]
                .bitcast(I32)
                .unsqueeze(0)
                .to_broadcast([8, 4, D // 4]),
            )
        nc.sync.dma_start(out=h_sb[:, tiles_of(2), :], in_=h_rows[:, tiles_of(2), :])
        nc.sync.dma_start(out=proto_sb[:], in_=prototypes)

        def warm_tensor_engine(count):
            for i in range(count):
                spare_ps = bank([P, P], F32, "spare_ps")
                nc.tensor.matmul(
                    out=spare_ps[:], lhsT=warm_ones[:], rhs=warm_ones[:], start=True, stop=True
                )

        def broadcast_bias():
            b3_ps = bank([P, D], F32, "b3_ps")
            nc.tensor.matmul(out=b3_ps[:], lhsT=ones_bf[:], rhs=b3_row[:], start=True, stop=True)
            return b3_ps

        def transpose_h(j):
            for t in range(PAIR * j, PAIR * (j + 1)):
                ht_ps[t] = bank([P, 2, P], F32, "ht_ps")
                words = h_sb[:, t, :].bitcast(F32)
                for w in range(2):
                    nc.tensor.transpose(ht_ps[t][:, w, :], words[:, w : H // 2 : 2], ident_f[:])

        def copy_h(j):
            for t in range(PAIR * j, PAIR * (j + 1)):
                nc.scalar.copy(
                    out=h_grouped[:, t, :, :].bitcast(F32),
                    in_=ht_ps[t][:].rearrange("p w r -> p r w"),
                )

        def quantise_h(tiles):
            nc.vector.quantize_mx(
                out=h_codes[:, tiles, :].rearrange("p i r -> p (i r)").bitcast(FP8X4),
                scales=h_scales[:, tiles, :].rearrange("p i r -> p (i r)"),
                in_=h_grouped[:, tiles, :, :].rearrange("p i r t -> p (i r t)"),
            )

        def first_matmul(t):
            u_ps[t] = bank([P, D], F32, "u_ps")
            nc.tensor.matmul_mx(
                out=u_ps[t][:],
                lhsT=h_codes[:, t, :].bitcast(FP8X4),
                lhsT_scale=h_scales[:, t, :],
                rhs=w_words[:].bitcast(FP4X4),
                rhs_scale=w_scales[:],
                start=True,
                stop=True,
            )

        def add_bias(t):
            nc.vector.tensor_tensor(out=u_sb[:, t, :], in0=u_ps[t][:], in1=b3_bc[:], op=ALU.add)

        def sum_squares(t):
            squares = scratch.tile([P, D], F32, name="squares")
            nc.scalar.activation(
                out=squares[:],
                in_=u_sb[:, t, :],
                func=ACT.Square,
                scale=SQRT_C,
                bias=u_floor[:],
                accum_out=sumsq[:, t : t + 1],
            )

        def norm_of_u(j):
            nc.gpsimd.tensor_tensor(
                out=inv_x[:, tiles_of(j)], in0=sumsq[:, tiles_of(j)], in1=minus_half[:], op=ALU.pow
            )

        def tanh_of_norm(j):
            for t in range(PAIR * j, PAIR * (j + 1)):
                nc.scalar.activation(
                    out=tanh_n[:, t : t + 1],
                    in_=sumsq[:, t : t + 1],
                    func=ACT.Tanh,
                    scale=inv_x[:, t : t + 1],
                )

        def hyp_of_tile(t, hyp):
            nc.vector.tensor_scalar(
                out=hyp[:, t, :],
                in0=u_sb[:, t, :],
                scalar1=tanh_n[:, t : t + 1],
                scalar2=inv_x[:, t : t + 1],
                op0=ALU.mult,
                op1=ALU.mult,
            )

        def hyp_of_u(j, hyp):
            for t in range(PAIR * j, PAIR * (j + 1)):
                hyp_of_tile(t, hyp)

        def store_hyp(j):
            nc.sync.dma_start(out=hyp_rows[:, tiles_of(j), :], in_=hyp_sb[:, tiles_of(j), :])

        def transpose_hyp(j):
            for t in range(PAIR * j, PAIR * (j + 1)):
                hypt_ps[t] = bank([P, 2, P], F32, "hypt_ps")
                words = hyp_bf[:, t, :].bitcast(F32)
                for w in range(2):
                    nc.tensor.transpose(
                        hypt_ps[t][:, w, :], words[:, w * P : (w + 1) * P], ident_f[:]
                    )

        def copy_hyp(t, copy):
            copy(
                out=hyp_grouped[:, t, :, :].bitcast(F32),
                in_=hypt_ps[t][:].rearrange("p w r -> p r w"),
            )

        def quantise_hyp(j):
            nc.vector.quantize_mx(
                out=hyp_codes[:, tiles_of(j), :].rearrange("p i r -> p (i r)").bitcast(FP8X4),
                scales=hyp_scales[:, tiles_of(j), :].rearrange("p i r -> p (i r)"),
                in_=hyp_grouped[:, tiles_of(j), :, :].rearrange("p i r t -> p (i r t)"),
            )

        def second_matmul(j):
            p_ps[j] = bank([P, PAIR, N], F32, "p_ps")
            for i in range(PAIR):
                nc.tensor.matmul_mx(
                    out=p_ps[j][:, i, :],
                    lhsT=hyp_codes[:, PAIR * j + i, :].bitcast(FP8X4),
                    lhsT_scale=hyp_scales[:, PAIR * j + i, :],
                    rhs=proto_codes[:].bitcast(FP8X4),
                    rhs_scale=proto_scales[:],
                    start=True,
                    stop=True,
                )

        def prototype_sums():
            squares = scratch.tile([P, D], F32, name="squares")
            nc.scalar.activation(out=squares[:], in_=proto_sb[:], func=ACT.Square, accum_out=a_col[:])

        def prototype_betas():
            nc.scalar.activation(
                out=beta_col[:], in_=a_col[:], func=ACT.Identity, scale=-C, bias=one_col[:]
            )

        def transpose_prototypes():
            protot_ps = bank([P, 2, N], F32, "protot_ps")
            words = proto_sb[:].bitcast(F32)
            for w in range(2):
                nc.tensor.transpose(protot_ps[:, w, :], words[:, w * P : (w + 1) * P], ident_f[:])
            return protot_ps

        def transpose_prototype_sums():
            rows_ps = bank([P, 2, N], F32, "rows_ps")
            for v, column in enumerate((a_col, beta_inv)):
                nc.tensor.transpose(
                    rows_ps[:, v, :], column[:, 0:1].to_broadcast([P, P]), ident_f[:]
                )
            return rows_ps

        def ball_norms(tiles):
            nc.scalar.activation(out=c_bn[:, tiles], in_=tanh_n[:, tiles], func=ACT.Square)

        def gamma_terms():
            nc.scalar.activation(
                out=gamma_raw[:], in_=c_bn[:], func=ACT.Identity, scale=-1.0, bias=one_col[:]
            )

        def sums_of_norms(j):
            for t in range(PAIR * j, PAIR * (j + 1)):
                nc.vector.tensor_scalar(
                    out=norm_sums[:, t, :],
                    in0=proto_rows[:, 0, :],
                    scalar1=C,
                    scalar2=c_bn[:, t : t + 1],
                    op0=ALU.mult,
                    op1=ALU.add,
                )

        def gap(j):
            nc.vector.scalar_tensor_tensor(
                out=c_gap[:, tiles_of(j), :],
                in0=p_ps[j][:],
                scalar=-2.0 * C,
                in1=norm_sums[:, tiles_of(j), :],
                op0=ALU.mult,
                op1=ALU.add,
            )

        def scale_gap(j):
            nc.vector.scalar_tensor_tensor(
                out=scaled_gap[:, tiles_of(j), :],
                in0=c_gap[:, tiles_of(j), :],
                scalar=MIN_NORM,
                in1=proto_rows[:, 1, :].unsqueeze(1).to_broadcast([P, PAIR, N]),
                op0=ALU.max,
                op1=ALU.mult,
            )

        def sinh_and_cosh(j):
            for t in range(PAIR * j, PAIR * (j + 1)):
                nc.scalar.activation(
                    out=sinh_t[:, t, :],
                    in_=scaled_gap[:, t, :],
                    func=ACT.Sqrt,
                    scale=gamma_inv[:, t : t + 1],
                )
                nc.scalar.activation(
                    out=cosh_t[:, t, :],
                    in_=scaled_gap[:, t, :],
                    func=ACT.Sqrt,
                    scale=gamma_inv[:, t : t + 1],
                    bias=one_col[:],
                )

        def exp_of_theta(j):
            nc.vector.tensor_tensor(
                out=exp_theta[:, tiles_of(j), :],
                in0=sinh_t[:, tiles_of(j), :],
                in1=cosh_t[:, tiles_of(j), :],
                op=ALU.add,
            )

        def logits(j):
            nc.scalar.activation(
                out=theta[:, tiles_of(j), :], in_=exp_theta[:, tiles_of(j), :], func=ACT.Ln
            )
            nc.vector.tensor_scalar(
                out=logit_sb[:, tiles_of(j), :],
                in0=theta[:, tiles_of(j), :],
                scalar1=LOGIT_SCALE,
                scalar2=LOGIT_SCALE * ARTANH_MAX,
                op0=ALU.mult,
                op1=ALU.max,
            )
            nc.sync.dma_start(out=logit_rows[:, tiles_of(j), :], in_=logit_sb[:, tiles_of(j), :])

        warm_tensor_engine(3)
        transpose_h(0)
        b3_ps = broadcast_bias()
        warm_tensor_engine(1)
        copy_h(0)
        quantise_h(slice(0, 1))
        quantise_h(slice(1, 2))
        transpose_h(1)
        nc.scalar.copy(out=b3_bc[:], in_=b3_ps[:])
        first_matmul(0)
        copy_h(1)
        transpose_h(2)
        first_matmul(1)
        protot_ps = transpose_prototypes()
        add_bias(0)
        quantise_h(tiles_of(1))
        copy_h(2)
        prototype_sums()
        add_bias(1)
        first_matmul(2)
        first_matmul(3)
        quantise_h(tiles_of(2))
        sum_squares(0)
        prototype_betas()
        add_bias(2)
        first_matmul(4)
        first_matmul(5)
        warm_tensor_engine(2)
        sum_squares(1)
        add_bias(3)
        norm_of_u(0)
        sum_squares(2)
        add_bias(4)
        sum_squares(3)
        add_bias(5)
        norm_of_u(1)
        tanh_of_norm(0)
        nc.vector.tensor_scalar_max(out=beta_floor[:], in0=beta_col[:], scalar1=BALL_EDGE)
        sum_squares(4)
        nc.vector.tensor_copy(
            out=proto_grouped[:].bitcast(F32), in_=protot_ps[:].rearrange("p w n -> p n w")
        )
        nc.vector.reciprocal(out=beta_inv[:], in_=beta_floor[:])
        rows_ps = transpose_prototype_sums()
        sum_squares(5)
        hyp_of_u(0, hyp_bf)
        tanh_of_norm(1)
        ball_norms(slice(0, 2 * PAIR))
        nc.vector.quantize_mx(
            out=proto_codes[:].bitcast(FP8X4),
            scales=proto_scales[:],
            in_=proto_grouped[:].rearrange("p n q -> p (n q)"),
        )
        hyp_of_u(1, hyp_bf)
        norm_of_u(2)
        nc.scalar.copy(out=proto_rows[:], in_=rows_ps[:])
        transpose_hyp(0)
        transpose_hyp(1)
        copy_hyp(0, nc.scalar.copy)
        tanh_of_norm(2)
        copy_hyp(1, nc.scalar.copy)
        ball_norms(tiles_of(2))
        nc.scalar.activation(
            out=shrink[:], in_=tanh_n[:, 0:1], func=ACT.Copy, scale=inv_x[:, 0:1]
        )
        copy_hyp(2, nc.scalar.copy)
        copy_hyp(3, nc.scalar.copy)
        gamma_terms()
        nc.scalar.activation(out=warm[:, 1:2], in_=one_col[:], func=ACT.Sqrt)
        sums_of_norms(0)
        sums_of_norms(1)
        quantise_hyp(0)
        second_matmul(0)
        hyp_of_u(2, hyp_bf)
        transpose_hyp(2)
        sums_of_norms(2)
        quantise_hyp(1)
        nc.vector.tensor_scalar_max(out=gamma[:], in0=gamma_raw[:], scalar1=BALL_EDGE)
        gap(0)
        copy_hyp(4, nc.vector.tensor_copy)
        copy_hyp(5, nc.vector.tensor_copy)
        nc.scalar.activation(
            out=hyp_sb[:, 0, :], in_=u_sb[:, 0, :], func=ACT.Copy, scale=shrink[:, 0:1]
        )
        second_matmul(1)
        nc.vector.reciprocal(out=gamma_inv[:], in_=gamma[:])
        scale_gap(0)
        quantise_hyp(2)
        second_matmul(2)
        gap(1)
        sinh_and_cosh(0)
        hyp_of_tile(1, hyp_sb)
        store_hyp(0)
        scale_gap(1)
        gap(2)
        sinh_and_cosh(1)
        hyp_of_tile(2, hyp_sb)
        scale_gap(2)
        sinh_and_cosh(2)
        hyp_of_tile(3, hyp_sb)
        store_hyp(1)
        exp_of_theta(0)
        hyp_of_u(2, hyp_sb)
        store_hyp(2)
        exp_of_theta(1)
        exp_of_theta(2)
        logits(0)
        logits(1)
        logits(2)
